import numpy as np
import ml_dtypes


def mxq(x, axis, fmt="e4m3"):
    dtype, down = {"e4m3": (ml_dtypes.float8_e4m3fn, 7), "e5m2": (ml_dtypes.float8_e5m2, 14)}[fmt]
    v = np.moveaxis(np.asarray(x, np.float32).astype(ml_dtypes.bfloat16).astype(np.float64), axis, -1)
    blocks = v.reshape(v.shape[:-1] + (-1, 32))
    amax = np.abs(blocks).max(-1, keepdims=True)
    byte = np.maximum(np.where(amax > 0, np.frexp(amax)[1] - 1 + 127, 0) - down, 1)
    scale = np.exp2(byte - 127.0)
    codes = (blocks / scale).astype(np.float32).astype(dtype).astype(np.float64)
    return np.moveaxis((codes * scale).reshape(v.shape), -1, axis)


WIDE = False


def mx_kscale(k):
    if not WIDE:
        return np.ones(k)
    levels = np.array([10, -10, 5, -5, 0])
    if k % 512:
        return np.exp2(np.random.permutation(np.resize(levels, k // 32))).repeat(32)
    a = np.empty((k // 512, 16))
    for p in range(k // 512):
        a[p, :8] = np.random.permutation(np.resize(levels, 8))
        for g in range(8):
            far = levels[np.abs(levels - a[p, g]) >= 10]
            a[p, g + 8] = far[np.random.randint(len(far))]
    return np.exp2(a.ravel()).repeat(32)


BF16 = ml_dtypes.bfloat16


def bf(x):
    return np.asarray(x, np.float32).astype(BF16)


def f64(x):
    return np.asarray(x).astype(np.float64)


B, T, C, KW = 2, 1024, 512, 3
PAD = KW // 2


def setup_inputs():
    s = mx_kscale(C)
    return {"x": bf(np.random.standard_normal((B, T, C)) * s),
            "w1": bf(np.random.standard_normal((C, C)) / np.sqrt(C) / s[None, :]),
            "b1": bf(np.random.standard_normal(C) * 0.2),
            "w2": bf(np.random.standard_normal((C, KW)) * 0.8),
            "b2": bf(np.random.standard_normal(C) * 0.2)}


def reference(x, w1, b1, w2, b2):
    h = (mxq(f64(x), 2, "e4m3") @ mxq(f64(w1), 1, "e4m3").T) + f64(b1)
    hp = np.pad(h, ((0, 0), (PAD, PAD), (0, 0)))
    taps = f64(w2)
    y = hp[:, 0:T, :] * taps[:, 0]
    for j in range(1, KW):
        y = y + hp[:, j:j + T, :] * taps[:, j]
    return y + f64(b2)

@@ -1,0 +1,215 @@
+from concourse import mybir
+from concourse.masks import make_identity
+
+F32 = mybir.dt.float32
+BF16 = mybir.dt.bfloat16
+U32 = mybir.dt.uint32
+U8 = mybir.dt.uint8
+FP8X4 = mybir.dt.float8_e4m3fn_x4
+MULT = mybir.AluOpType.mult
+ADD = mybir.AluOpType.add
+SUBTRACT = mybir.AluOpType.subtract
+IDENTITY = mybir.ActivationFunctionType.Identity
+
+B, T, C, KW = 2, 1024, 512, 3
+P = 128
+PACK = 4
+HALVES = 2
+WORDS = C // 2
+CHUNK = 512
+ROW_BLOCKS = CHUNK // P
+D_BLOCKS = C // P
+CHUNKS = T // CHUNK
+AHEAD = 2
+WARM = 5
+
+FLOPS = 2 * B * T * C * C + 2 * KW * B * T * C
+
+
+def tile_cvim_pa_kernel(tc, x, w1, b1, w2, b2, out):
+    nc = tc.nc
+
+    with (
+        tc.tile_pool(name="keep", bufs=1) as keep,
+        tc.tile_pool(name="stage", bufs=3) as stage,
+        tc.tile_pool(name="work", bufs=AHEAD + 3) as work,
+        tc.tile_pool(name="leave", bufs=8) as leave,
+        tc.psum_pool(name="psum", bufs=(AHEAD + 1) * CHUNKS) as psum,
+        tc.psum_pool(name="psum_back", bufs=2) as psum_back,
+        tc.manual_schedule(),
+    ):
+        zeros = keep.tile([P, CHUNK], BF16)
+        nc.vector.memset(zeros[:], 0.0)
+        unread = psum.tile([P, CHUNK], F32, tag="bank")
+        for k in range(WARM):
+            nc.tensor.matmul(out=unread[:], lhsT=zeros[:, 0:P], rhs=zeros[:], start=True, stop=True)
+
+        taps_bf = keep.tile([P, D_BLOCKS, KW], BF16)
+        b1_bf = keep.tile([P, D_BLOCKS], BF16)
+        b2_bf = keep.tile([P, D_BLOCKS], BF16)
+        with nc.allow_non_contiguous_dma(reason="one value of a 512-long vector to a partition"):
+            nc.scalar.dma_start(out=taps_bf[:], in_=w2.rearrange("(m p) j -> p m j", p=P))
+            nc.scalar.dma_start(out=b1_bf[:], in_=b1.rearrange("(m p) -> p m", p=P))
+            nc.scalar.dma_start(out=b2_bf[:], in_=b2.rearrange("(m p) -> p m", p=P))
+
+        def load_rows(rows_dram, name):
+            rows = keep.tile([P, ROW_BLOCKS * C], BF16, name=name)
+            for pair in range(ROW_BLOCKS // 2):
+                nc.sync.dma_start(
+                    out=rows[:, 2 * pair * C : (2 * pair + 2) * C].rearrange("p (r c) -> p r c", c=C),
+                    in_=rows_dram[2 * pair * P : (2 * pair + 2) * P, :].rearrange("(r p) c -> p r c", p=P),
+                )
+            return rows
+
+        w_rows = load_rows(w1, "w_rows")
+        x_rows = {}
+        for b in range(B):
+            for n in range(CHUNKS):
+                x_rows[b, n] = load_rows(x[b, n * CHUNK : (n + 1) * CHUNK, :], "x_rows_%d_%d" % (b, n))
+
+        ident = keep.tile([P, P], F32)
+        make_identity(nc, ident[:])
+
+        taps = keep.tile([P, D_BLOCKS, KW], F32)
+        nc.gpsimd.tensor_copy(out=taps[:], in_=taps_bf[:])
+        tap_bias = keep.tile([P, D_BLOCKS, KW], F32)
+        nc.gpsimd.tensor_tensor(
+            out=tap_bias[:],
+            in0=taps[:],
+            in1=b1_bf[:].unsqueeze(2).to_broadcast([P, D_BLOCKS, KW]),
+            op=MULT,
+        )
+        inner_bias = keep.tile([P, D_BLOCKS], F32)
+        nc.gpsimd.tensor_tensor(out=inner_bias[:], in0=tap_bias[:, :, 0], in1=b2_bf[:], op=ADD)
+        for j in range(1, KW):
+            nc.gpsimd.tensor_tensor(out=inner_bias[:], in0=inner_bias[:], in1=tap_bias[:, :, j], op=ADD)
+
+        def regroup_rows(rows):
+            words = rows[:].bitcast(F32)
+            grouped = stage.tile([P, CHUNK * PACK], BF16, align_bytes=64)
+            grouped_words = grouped[:].bitcast(F32).rearrange("p (t u) -> p t u", u=HALVES)
+            for pair in range(ROW_BLOCKS // 2):
+                flipped = psum.tile([P, HALVES, 2 * P], F32, tag="bank")
+                for r in (2 * pair, 2 * pair + 1):
+                    for u in range(HALVES):
+                        nc.tensor.transpose(
+                            flipped[:, u, (r % 2) * P : (r % 2 + 1) * P],
+                            words[:, r * WORDS + u : (r + 1) * WORDS : HALVES],
+                            ident[:],
+                        )
+                nc.scalar.copy(
+                    out=grouped_words[:, 2 * pair * P : (2 * pair + 2) * P, :],
+                    in_=flipped[:].rearrange("p u t -> p t u"),
+                )
+            return grouped
+
+        w_codes = keep.tile([P, C], U32, align_bytes=64)
+        w_scales = keep.tile([P, C], U8, align_bytes=64)
+        x_codes = keep.tile([P, B, CHUNKS, CHUNK], U32, align_bytes=64)
+        x_scales = keep.tile([P, B, CHUNKS, CHUNK], U8, align_bytes=64)
+        sources = [(w_rows, w_codes[:], w_scales[:])]
+        for b in range(B):
+            for n in range(CHUNKS):
+                sources.append((x_rows[b, n], x_codes[:, b, n, :], x_scales[:, b, n, :]))
+        grouped_tiles = []
+
+        def quantise(k):
+            rows, codes, scales = sources[k]
+            nc.vector.quantize_mx(out=codes.bitcast(FP8X4), scales=scales, in_=grouped_tiles[k][:])
+
+        for k in range(len(sources) - 1):
+            grouped_tiles.append(regroup_rows(sources[k][0]))
+            quantise(k)
+
+        acc = {}
+        y_cols = {}
+
+        def middle_tap(b, m):
+            y = work.tile([P, T], F32, name="y_cols")
+            y_cols[b, m] = y
+            for n in range(CHUNKS):
+                acc[b, m, n] = psum.tile([P, CHUNK], F32, name="acc", tag="bank")
+                nc.tensor.matmul_mx(
+                    out=acc[b, m, n][:],
+                    lhsT=w_codes[:, m * P : (m + 1) * P].bitcast(FP8X4),
+                    lhsT_scale=w_scales[:, m * P : (m + 1) * P],
+                    rhs=x_codes[:, b, n, :].bitcast(FP8X4),
+                    rhs_scale=x_scales[:, b, n, :],
+                    start=True,
+                    stop=True,
+                )
+            for n in range(CHUNKS):
+                nc.scalar.activation(
+                    out=y[:, n * CHUNK : (n + 1) * CHUNK],
+                    in_=acc[b, m, n][:],
+                    func=IDENTITY,
+                    scale=taps[:, m, 1:2],
+                    bias=inner_bias[:, m : m + 1],
+                )
+            nc.gpsimd.tensor_tensor(
+                out=y[:, 0 : T : T - 1],
+                in0=y[:, 0 : T : T - 1],
+                in1=tap_bias[:, m, 0 : KW : KW - 1],
+                op=SUBTRACT,
+            )
+
+        def right_tap(b, m, n):
+            y = y_cols[b, m]
+            t0 = n * CHUNK
+            skip = 1 if n == 0 else 0
+            nc.vector.scalar_tensor_tensor(
+                out=y[:, t0 - 1 + skip : t0 + CHUNK - 1],
+                in0=acc[b, m, n][:, skip:CHUNK],
+                scalar=taps[:, m, 2:3],
+                in1=y[:, t0 - 1 + skip : t0 + CHUNK - 1],
+                op0=MULT,
+                op1=ADD,
+            )
+
+        def left_tap(b, m, n):
+            y = y_cols[b, m]
+            t0 = n * CHUNK
+            width = min(CHUNK, T - 1 - t0)
+            nc.vector.scalar_tensor_tensor(
+                out=y[:, t0 + 1 : t0 + 1 + width],
+                in0=acc[b, m, n][:, 0:width],
+                scalar=taps[:, m, 0:1],
+                in1=y[:, t0 + 1 : t0 + 1 + width],
+                op0=MULT,
+                op1=ADD,
+            )
+
+        def store_unit(b, m):
+            for n in range(CHUNKS):
+                y_rows_ps = psum_back.tile([P, ROW_BLOCKS, P], F32)
+                for k in range(ROW_BLOCKS):
+                    t0 = n * CHUNK + k * P
+                    nc.tensor.transpose(y_rows_ps[:, k, :], y_cols[b, m][:, t0 : t0 + P], ident[:])
+                y_rows = leave.tile([P, ROW_BLOCKS, P], F32)
+                nc.scalar.copy(out=y_rows[:], in_=y_rows_ps[:])
+                nc.sync.dma_start(
+                    out=out[b, n * CHUNK : (n + 1) * CHUNK, m * P : (m + 1) * P].rearrange(
+                        "(k p) d -> p k d", p=P
+                    ),
+                    in_=y_rows[:],
+                )
+
+        units = [(b, m) for b in range(B) for m in range(D_BLOCKS)]
+        for unit in units[:AHEAD]:
+            middle_tap(*unit)
+        grouped_tiles.append(regroup_rows(sources[-1][0]))
+        right_tap(*units[0], 0)
+        for i, unit in enumerate(units):
+            if i + AHEAD < len(units):
+                middle_tap(*units[i + AHEAD])
+            for n in range(1, CHUNKS):
+                right_tap(*unit, n)
+            if i + 1 < len(units):
+                right_tap(*units[i + 1], 0)
+            for n in range(CHUNKS):
+                left_tap(*unit, n)
+            if i == 0:
+                quantise(len(sources) - 1)
+            if i > 0:
+                store_unit(*units[i - 1])
+        store_unit(*units[-1])

@@ -20,6 +20,8 @@ CHUNK = 512
 ROW_BLOCKS = CHUNK // P
 D_BLOCKS = C // P
 CHUNKS = T // CHUNK
+PAIR = 2 * P
+PAIRS = CHUNK // PAIR
 AHEAD = 2
 WARM = 5
 
@@ -31,11 +33,10 @@ def tile_cvim_pa_kernel(tc, x, w1, b1, w2, b2, out):
 
     with (
         tc.tile_pool(name="keep", bufs=1) as keep,
-        tc.tile_pool(name="stage", bufs=3) as stage,
         tc.tile_pool(name="work", bufs=AHEAD + 3) as work,
         tc.tile_pool(name="leave", bufs=8) as leave,
         tc.psum_pool(name="psum", bufs=(AHEAD + 1) * CHUNKS) as psum,
-        tc.psum_pool(name="psum_back", bufs=2) as psum_back,
+        tc.psum_pool(name="psum_turn", bufs=2) as psum_turn,
         tc.manual_schedule(),
     ):
         zeros = keep.tile([P, CHUNK], BF16)
@@ -52,20 +53,36 @@ def tile_cvim_pa_kernel(tc, x, w1, b1, w2, b2, out):
             nc.scalar.dma_start(out=b1_bf[:], in_=b1.rearrange("(m p) -> p m", p=P))
             nc.scalar.dma_start(out=b2_bf[:], in_=b2.rearrange("(m p) -> p m", p=P))
 
-        def load_rows(rows_dram, name):
-            rows = keep.tile([P, ROW_BLOCKS * C], BF16, name=name)
-            for pair in range(ROW_BLOCKS // 2):
-                nc.sync.dma_start(
-                    out=rows[:, 2 * pair * C : (2 * pair + 2) * C].rearrange("p (r c) -> p r c", c=C),
-                    in_=rows_dram[2 * pair * P : (2 * pair + 2) * P, :].rearrange("(r p) c -> p r c", p=P),
-                )
-            return rows
+        W = 0
 
-        w_rows = load_rows(w1, "w_rows")
-        x_rows = {}
+        def chunk_source(b, n):
+            return 1 + CHUNKS * b + n
+
+        row_tiles, grouped_tiles, codes, scales, drams = [], [], [], [], []
+        for k in range(1 + B * CHUNKS):
+            row_tiles.append(keep.tile([P, ROW_BLOCKS, C], BF16, name="rows_%d" % k))
+            grouped_tiles.append(keep.tile([P, CHUNK * PACK], BF16, align_bytes=64, name="grouped_%d" % k))
+            codes.append(keep.tile([P, CHUNK], U32, align_bytes=64, name="codes_%d" % k))
+            scales.append(keep.tile([P, CHUNK], U8, align_bytes=64, name="scales_%d" % k))
+        drams.append(w1)
         for b in range(B):
             for n in range(CHUNKS):
-                x_rows[b, n] = load_rows(x[b, n * CHUNK : (n + 1) * CHUNK, :], "x_rows_%d_%d" % (b, n))
+                drams.append(x[b, n * CHUNK : (n + 1) * CHUNK, :])
+
+        def load(k, pair):
+            nc.sync.dma_start(
+                out=row_tiles[k][:, 2 * pair : 2 * pair + 2, :],
+                in_=drams[k][pair * PAIR : (pair + 1) * PAIR, :].rearrange("(r p) c -> p r c", p=P),
+            )
+
+        load(W, 0)
+        for n in range(CHUNKS):
+            for pair in range(PAIRS):
+                load(chunk_source(0, n), pair)
+        load(W, 1)
+        for n in range(CHUNKS):
+            for pair in range(PAIRS):
+                load(chunk_source(1, n), pair)
 
         ident = keep.tile([P, P], F32)
         make_identity(nc, ident[:])
@@ -84,68 +101,58 @@ def tile_cvim_pa_kernel(tc, x, w1, b1, w2, b2, out):
         for j in range(1, KW):
             nc.gpsimd.tensor_tensor(out=inner_bias[:], in0=inner_bias[:], in1=tap_bias[:, :, j], op=ADD)
 
-        def regroup_rows(rows):
-            words = rows[:].bitcast(F32)
-            grouped = stage.tile([P, CHUNK * PACK], BF16, align_bytes=64)
-            grouped_words = grouped[:].bitcast(F32).rearrange("p (t u) -> p t u", u=HALVES)
-            for pair in range(ROW_BLOCKS // 2):
-                flipped = psum.tile([P, HALVES, 2 * P], F32, tag="bank")
-                for r in (2 * pair, 2 * pair + 1):
-                    for u in range(HALVES):
-                        nc.tensor.transpose(
-                            flipped[:, u, (r % 2) * P : (r % 2 + 1) * P],
-                            words[:, r * WORDS + u : (r + 1) * WORDS : HALVES],
-                            ident[:],
-                        )
-                nc.scalar.copy(
-                    out=grouped_words[:, 2 * pair * P : (2 * pair + 2) * P, :],
-                    in_=flipped[:].rearrange("p u t -> p t u"),
-                )
-            return grouped
+        def turn(k, pair, copy, banks, tag):
+            words = row_tiles[k][:].rearrange("p r c -> p (r c)").bitcast(F32)
+            flipped = banks.tile([P, HALVES, PAIR], F32, name="flipped", tag=tag)
+            for r in range(2):
+                row_block = 2 * pair + r
+                for u in range(HALVES):
+                    nc.tensor.transpose(
+                        flipped[:, u, r * P : (r + 1) * P],
+                        words[:, row_block * WORDS + u : (row_block + 1) * WORDS : HALVES],
+                        ident[:],
+                    )
+            copy(
+                out=grouped_tiles[k][:].bitcast(F32).rearrange("p (t u) -> p t u", u=HALVES)[
+                    :, pair * PAIR : (pair + 1) * PAIR, :
+                ],
+                in_=flipped[:].rearrange("p u t -> p t u"),
+            )
 
-        w_codes = keep.tile([P, C], U32, align_bytes=64)
-        w_scales = keep.tile([P, C], U8, align_bytes=64)
-        x_codes = keep.tile([P, B, CHUNKS, CHUNK], U32, align_bytes=64)
-        x_scales = keep.tile([P, B, CHUNKS, CHUNK], U8, align_bytes=64)
-        sources = [(w_rows, w_codes[:], w_scales[:])]
-        for b in range(B):
-            for n in range(CHUNKS):
-                sources.append((x_rows[b, n], x_codes[:, b, n, :], x_scales[:, b, n, :]))
-        grouped_tiles = []
-
-        def quantise(k):
-            rows, codes, scales = sources[k]
-            nc.vector.quantize_mx(out=codes.bitcast(FP8X4), scales=scales, in_=grouped_tiles[k][:])
-
-        for k in range(len(sources) - 1):
-            grouped_tiles.append(regroup_rows(sources[k][0]))
-            quantise(k)
+        def quantise(k, first_pair=0, pairs=PAIRS):
+            rows = slice(first_pair * PAIR, (first_pair + pairs) * PAIR)
+            nc.vector.quantize_mx(
+                out=codes[k][:, rows].bitcast(FP8X4),
+                scales=scales[k][:, rows],
+                in_=grouped_tiles[k][:, rows.start * PACK : rows.stop * PACK],
+            )
 
         acc = {}
         y_cols = {}
 
-        def middle_tap(b, m):
-            y = work.tile([P, T], F32, name="y_cols")
-            y_cols[b, m] = y
-            for n in range(CHUNKS):
-                acc[b, m, n] = psum.tile([P, CHUNK], F32, name="acc", tag="bank")
-                nc.tensor.matmul_mx(
-                    out=acc[b, m, n][:],
-                    lhsT=w_codes[:, m * P : (m + 1) * P].bitcast(FP8X4),
-                    lhsT_scale=w_scales[:, m * P : (m + 1) * P],
-                    rhs=x_codes[:, b, n, :].bitcast(FP8X4),
-                    rhs_scale=x_scales[:, b, n, :],
-                    start=True,
-                    stop=True,
-                )
-            for n in range(CHUNKS):
-                nc.scalar.activation(
-                    out=y[:, n * CHUNK : (n + 1) * CHUNK],
-                    in_=acc[b, m, n][:],
-                    func=IDENTITY,
-                    scale=taps[:, m, 1:2],
-                    bias=inner_bias[:, m : m + 1],
-                )
+        def middle_tap(b, m, n):
+            if n == 0:
+                y_cols[b, m] = work.tile([P, T], F32, name="y_cols")
+            acc[b, m, n] = psum.tile([P, CHUNK], F32, name="acc", tag="bank")
+            nc.tensor.matmul_mx(
+                out=acc[b, m, n][:],
+                lhsT=codes[W][:, m * P : (m + 1) * P].bitcast(FP8X4),
+                lhsT_scale=scales[W][:, m * P : (m + 1) * P],
+                rhs=codes[chunk_source(b, n)][:].bitcast(FP8X4),
+                rhs_scale=scales[chunk_source(b, n)][:],
+                start=True,
+                stop=True,
+            )
+            nc.scalar.activation(
+                out=y_cols[b, m][:, n * CHUNK : (n + 1) * CHUNK],
+                in_=acc[b, m, n][:],
+                func=IDENTITY,
+                scale=taps[:, m, 1:2],
+                bias=inner_bias[:, m : m + 1],
+            )
+
+        def end_bias(b, m):
+            y = y_cols[b, m]
             nc.gpsimd.tensor_tensor(
                 out=y[:, 0 : T : T - 1],
                 in0=y[:, 0 : T : T - 1],
@@ -179,37 +186,59 @@ def tile_cvim_pa_kernel(tc, x, w1, b1, w2, b2, out):
                 op1=ADD,
             )
 
-        def store_unit(b, m):
-            for n in range(CHUNKS):
-                y_rows_ps = psum_back.tile([P, ROW_BLOCKS, P], F32)
-                for k in range(ROW_BLOCKS):
-                    t0 = n * CHUNK + k * P
-                    nc.tensor.transpose(y_rows_ps[:, k, :], y_cols[b, m][:, t0 : t0 + P], ident[:])
-                y_rows = leave.tile([P, ROW_BLOCKS, P], F32)
-                nc.scalar.copy(out=y_rows[:], in_=y_rows_ps[:])
-                nc.sync.dma_start(
-                    out=out[b, n * CHUNK : (n + 1) * CHUNK, m * P : (m + 1) * P].rearrange(
-                        "(k p) d -> p k d", p=P
-                    ),
-                    in_=y_rows[:],
-                )
+        def store_chunk(b, m, n, copy):
+            y_rows_ps = psum_turn.tile([P, ROW_BLOCKS, P], F32, name="y_rows_ps", tag="turn")
+            for k in range(ROW_BLOCKS):
+                t0 = n * CHUNK + k * P
+                nc.tensor.transpose(y_rows_ps[:, k, :], y_cols[b, m][:, t0 : t0 + P], ident[:])
+            y_rows = leave.tile([P, ROW_BLOCKS, P], F32)
+            copy(out=y_rows[:], in_=y_rows_ps[:])
+            nc.sync.dma_start(
+                out=out[b, n * CHUNK : (n + 1) * CHUNK, m * P : (m + 1) * P].rearrange("(k p) d -> p k d", p=P),
+                in_=y_rows[:],
+            )
 
+        scalar_copy = nc.scalar.copy
+        vector_copy = nc.vector.tensor_copy
         units = [(b, m) for b in range(B) for m in range(D_BLOCKS)]
+
+        early = (psum, "bank")
+        turn(W, 0, scalar_copy, *early)
+        turn(chunk_source(0, 0), 0, vector_copy, *early)
+        turn(chunk_source(0, 0), 1, scalar_copy, *early)
+        quantise(W, 0, 1)
+        for pair in range(PAIRS):
+            turn(chunk_source(0, 1), pair, scalar_copy, *early)
+        quantise(chunk_source(0, 0))
+        turn(W, 1, vector_copy, *early)
         for unit in units[:AHEAD]:
-            middle_tap(*unit)
-        grouped_tiles.append(regroup_rows(sources[-1][0]))
+            middle_tap(*unit, 0)
+        quantise(chunk_source(0, 1))
+        for unit in units[:AHEAD]:
+            middle_tap(*unit, 1)
         right_tap(*units[0], 0)
+        quantise(W, 1, 1)
+
         for i, unit in enumerate(units):
+            right_tap(*unit, 1)
             if i + AHEAD < len(units):
-                middle_tap(*units[i + AHEAD])
-            for n in range(1, CHUNKS):
-                right_tap(*unit, n)
+                for n in range(CHUNKS):
+                    middle_tap(*units[i + AHEAD], n)
+                if i + AHEAD >= 2 * AHEAD:
+                    end_bias(*units[i + AHEAD])
+            if i < CHUNKS:
+                for pair in range(PAIRS):
+                    turn(chunk_source(1, i), pair, scalar_copy, psum_turn, "turn")
             if i + 1 < len(units):
                 right_tap(*units[i + 1], 0)
             for n in range(CHUNKS):
                 left_tap(*unit, n)
-            if i == 0:
-                quantise(len(sources) - 1)
+            if i < 2 * AHEAD:
+                end_bias(*unit)
+            if i < CHUNKS:
+                quantise(chunk_source(1, i))
             if i > 0:
-                store_unit(*units[i - 1])
-        store_unit(*units[-1])
+                for n in range(CHUNKS):
+                    store_chunk(*units[i - 1], n, scalar_copy)
+        store_chunk(*units[-1], 0, scalar_copy)
+        store_chunk(*units[-1], 1, vector_copy)

@@ -45,13 +45,15 @@ def tile_cvim_pa_kernel(tc, x, w1, b1, w2, b2, out):
         for k in range(WARM):
             nc.tensor.matmul(out=unread[:], lhsT=zeros[:, 0:P], rhs=zeros[:], start=True, stop=True)
 
-        taps_bf = keep.tile([P, D_BLOCKS, KW], BF16)
-        b1_bf = keep.tile([P, D_BLOCKS], BF16)
-        b2_bf = keep.tile([P, D_BLOCKS], BF16)
-        with nc.allow_non_contiguous_dma(reason="one value of a 512-long vector to a partition"):
-            nc.scalar.dma_start(out=taps_bf[:], in_=w2.rearrange("(m p) j -> p m j", p=P))
-            nc.scalar.dma_start(out=b1_bf[:], in_=b1.rearrange("(m p) -> p m", p=P))
-            nc.scalar.dma_start(out=b2_bf[:], in_=b2.rearrange("(m p) -> p m", p=P))
+        small_rows = keep.tile([P, (KW + 2) * P], BF16)
+        nc.gpsimd.memset(small_rows[:], 0.0)
+        nc.scalar.dma_start(out=small_rows[0:D_BLOCKS, 0 : KW * P], in_=w2.rearrange("(m p) j -> m (p j)", p=P))
+        nc.scalar.dma_start(out=small_rows[0:D_BLOCKS, KW * P : (KW + 1) * P], in_=b1.rearrange("(m p) -> m p", p=P))
+        nc.scalar.dma_start(out=small_rows[0:D_BLOCKS, (KW + 1) * P :], in_=b2.rearrange("(m p) -> m p", p=P))
+        ident = keep.tile([P, P], F32)
+        make_identity(nc, ident[:])
+        ident_bf = keep.tile([P, P], BF16)
+        nc.vector.tensor_copy(out=ident_bf[:], in_=ident[:])
 
         W = 0
 
@@ -60,7 +62,7 @@ def tile_cvim_pa_kernel(tc, x, w1, b1, w2, b2, out):
 
         row_tiles, grouped_tiles, codes, scales, drams = [], [], [], [], []
         for k in range(1 + B * CHUNKS):
-            row_tiles.append(keep.tile([P, ROW_BLOCKS, C], BF16, name="rows_%d" % k))
+            row_tiles.append(keep.tile([P, ROW_BLOCKS * C], BF16, name="rows_%d" % k))
             grouped_tiles.append(keep.tile([P, CHUNK * PACK], BF16, align_bytes=64, name="grouped_%d" % k))
             codes.append(keep.tile([P, CHUNK], U32, align_bytes=64, name="codes_%d" % k))
             scales.append(keep.tile([P, CHUNK], U8, align_bytes=64, name="scales_%d" % k))
@@ -71,8 +73,8 @@ def tile_cvim_pa_kernel(tc, x, w1, b1, w2, b2, out):
 
         def load(k, pair):
             nc.sync.dma_start(
-                out=row_tiles[k][:, 2 * pair : 2 * pair + 2, :],
-                in_=drams[k][pair * PAIR : (pair + 1) * PAIR, :].rearrange("(r p) c -> p r c", p=P),
+                out=row_tiles[k][:, 2 * pair * C : (2 * pair + 2) * C],
+                in_=drams[k][pair * PAIR : (pair + 1) * PAIR, :].rearrange("(p r) c -> p (r c)", r=2),
             )
 
         load(W, 0)
@@ -84,25 +86,8 @@ def tile_cvim_pa_kernel(tc, x, w1, b1, w2, b2, out):
             for pair in range(PAIRS):
                 load(chunk_source(1, n), pair)
 
-        ident = keep.tile([P, P], F32)
-        make_identity(nc, ident[:])
-
-        taps = keep.tile([P, D_BLOCKS, KW], F32)
-        nc.gpsimd.tensor_copy(out=taps[:], in_=taps_bf[:])
-        tap_bias = keep.tile([P, D_BLOCKS, KW], F32)
-        nc.gpsimd.tensor_tensor(
-            out=tap_bias[:],
-            in0=taps[:],
-            in1=b1_bf[:].unsqueeze(2).to_broadcast([P, D_BLOCKS, KW]),
-            op=MULT,
-        )
-        inner_bias = keep.tile([P, D_BLOCKS], F32)
-        nc.gpsimd.tensor_tensor(out=inner_bias[:], in0=tap_bias[:, :, 0], in1=b2_bf[:], op=ADD)
-        for j in range(1, KW):
-            nc.gpsimd.tensor_tensor(out=inner_bias[:], in0=inner_bias[:], in1=tap_bias[:, :, j], op=ADD)
-
         def turn(k, pair, copy, banks, tag):
-            words = row_tiles[k][:].rearrange("p r c -> p (r c)").bitcast(F32)
+            words = row_tiles[k][:].bitcast(F32)
             flipped = banks.tile([P, HALVES, PAIR], F32, name="flipped", tag=tag)
             for r in range(2):
                 row_block = 2 * pair + r
@@ -113,10 +98,10 @@ def tile_cvim_pa_kernel(tc, x, w1, b1, w2, b2, out):
                         ident[:],
                     )
             copy(
-                out=grouped_tiles[k][:].bitcast(F32).rearrange("p (t u) -> p t u", u=HALVES)[
-                    :, pair * PAIR : (pair + 1) * PAIR, :
-                ],
-                in_=flipped[:].rearrange("p u t -> p t u"),
+                out=grouped_tiles[k][:]
+                .bitcast(F32)[:, pair * PAIR * HALVES : (pair + 1) * PAIR * HALVES]
+                .rearrange("p (t r u) -> p t r u", r=2, u=HALVES),
+                in_=flipped[:].rearrange("p u (r t) -> p t r u", r=2),
             )
 
         def quantise(k, first_pair=0, pairs=PAIRS):
@@ -126,6 +111,27 @@ def tile_cvim_pa_kernel(tc, x, w1, b1, w2, b2, out):
                 scales=scales[k][:, rows],
                 in_=grouped_tiles[k][:, rows.start * PACK : rows.stop * PACK],
             )
+
+        cols = keep.tile([P, KW + 2, D_BLOCKS], F32)
+        tap_bias = keep.tile([P, KW, D_BLOCKS], F32)
+        inner_bias = keep.tile([P, D_BLOCKS], F32)
+
+        def turn_small():
+            small_ps = psum.tile([P, KW + 2, P], BF16, name="small_ps", tag="bank")
+            views = [small_rows[:, j : KW * P : KW] for j in range(KW)]
+            views += [small_rows[:, KW * P : (KW + 1) * P], small_rows[:, (KW + 1) * P :]]
+            for j, view in enumerate(views):
+                nc.tensor.transpose(small_ps[:, j, :], view, ident_bf[:])
+            nc.vector.tensor_copy(out=cols[:], in_=small_ps[:, :, 0:D_BLOCKS])
+            nc.gpsimd.tensor_tensor(
+                out=tap_bias[:],
+                in0=cols[:, 0:KW, :],
+                in1=cols[:, KW : KW + 1, :].to_broadcast([P, KW, D_BLOCKS]),
+                op=MULT,
+            )
+            nc.gpsimd.tensor_tensor(out=inner_bias[:], in0=tap_bias[:, 0, :], in1=cols[:, KW + 1, :], op=ADD)
+            for j in range(1, KW):
+                nc.gpsimd.tensor_tensor(out=inner_bias[:], in0=inner_bias[:], in1=tap_bias[:, j, :], op=ADD)
 
         acc = {}
         y_cols = {}
@@ -147,7 +153,7 @@ def tile_cvim_pa_kernel(tc, x, w1, b1, w2, b2, out):
                 out=y_cols[b, m][:, n * CHUNK : (n + 1) * CHUNK],
                 in_=acc[b, m, n][:],
                 func=IDENTITY,
-                scale=taps[:, m, 1:2],
+                scale=cols[:, 1, m : m + 1],
                 bias=inner_bias[:, m : m + 1],
             )
 
@@ -156,7 +162,7 @@ def tile_cvim_pa_kernel(tc, x, w1, b1, w2, b2, out):
             nc.gpsimd.tensor_tensor(
                 out=y[:, 0 : T : T - 1],
                 in0=y[:, 0 : T : T - 1],
-                in1=tap_bias[:, m, 0 : KW : KW - 1],
+                in1=tap_bias[:, 0 : KW : KW - 1, m],
                 op=SUBTRACT,
             )
 
@@ -167,7 +173,7 @@ def tile_cvim_pa_kernel(tc, x, w1, b1, w2, b2, out):
             nc.vector.scalar_tensor_tensor(
                 out=y[:, t0 - 1 + skip : t0 + CHUNK - 1],
                 in0=acc[b, m, n][:, skip:CHUNK],
-                scalar=taps[:, m, 2:3],
+                scalar=cols[:, 2, m : m + 1],
                 in1=y[:, t0 - 1 + skip : t0 + CHUNK - 1],
                 op0=MULT,
                 op1=ADD,
@@ -180,14 +186,14 @@ def tile_cvim_pa_kernel(tc, x, w1, b1, w2, b2, out):
             nc.vector.scalar_tensor_tensor(
                 out=y[:, t0 + 1 : t0 + 1 + width],
                 in0=acc[b, m, n][:, 0:width],
-                scalar=taps[:, m, 0:1],
+                scalar=cols[:, 0, m : m + 1],
                 in1=y[:, t0 + 1 : t0 + 1 + width],
                 op0=MULT,
                 op1=ADD,
             )
 
-        def store_chunk(b, m, n, copy):
-            y_rows_ps = psum_turn.tile([P, ROW_BLOCKS, P], F32, name="y_rows_ps", tag="turn")
+        def store_chunk(b, m, n, copy, banks, tag):
+            y_rows_ps = banks.tile([P, ROW_BLOCKS, P], F32, name="y_rows_ps", tag=tag)
             for k in range(ROW_BLOCKS):
                 t0 = n * CHUNK + k * P
                 nc.tensor.transpose(y_rows_ps[:, k, :], y_cols[b, m][:, t0 : t0 + P], ident[:])
@@ -202,15 +208,17 @@ def tile_cvim_pa_kernel(tc, x, w1, b1, w2, b2, out):
         vector_copy = nc.vector.tensor_copy
         units = [(b, m) for b in range(B) for m in range(D_BLOCKS)]
 
-        early = (psum, "bank")
-        turn(W, 0, scalar_copy, *early)
-        turn(chunk_source(0, 0), 0, vector_copy, *early)
-        turn(chunk_source(0, 0), 1, scalar_copy, *early)
+        sum_banks = (psum, "bank")
+        turn_banks = (psum_turn, "turn")
+        turn(W, 0, scalar_copy, *sum_banks)
+        turn_small()
+        turn(chunk_source(0, 0), 0, scalar_copy, *sum_banks)
+        turn(chunk_source(0, 0), 1, scalar_copy, *sum_banks)
         quantise(W, 0, 1)
         for pair in range(PAIRS):
-            turn(chunk_source(0, 1), pair, scalar_copy, *early)
+            turn(chunk_source(0, 1), pair, scalar_copy, *sum_banks)
         quantise(chunk_source(0, 0))
-        turn(W, 1, vector_copy, *early)
+        turn(W, 1, scalar_copy, *sum_banks)
         for unit in units[:AHEAD]:
             middle_tap(*unit, 0)
         quantise(chunk_source(0, 1))
@@ -221,24 +229,27 @@ def tile_cvim_pa_kernel(tc, x, w1, b1, w2, b2, out):
 
         for i, unit in enumerate(units):
             right_tap(*unit, 1)
+            if i == 1:
+                quantise(chunk_source(1, 0))
             if i + AHEAD < len(units):
                 for n in range(CHUNKS):
                     middle_tap(*units[i + AHEAD], n)
-                if i + AHEAD >= 2 * AHEAD:
+                if i + AHEAD + 1 == len(units):
                     end_bias(*units[i + AHEAD])
             if i < CHUNKS:
                 for pair in range(PAIRS):
-                    turn(chunk_source(1, i), pair, scalar_copy, psum_turn, "turn")
+                    turn(chunk_source(1, i), pair, scalar_copy, *turn_banks)
             if i + 1 < len(units):
                 right_tap(*units[i + 1], 0)
             for n in range(CHUNKS):
                 left_tap(*unit, n)
-            if i < 2 * AHEAD:
+            if i + 1 < len(units):
                 end_bias(*unit)
-            if i < CHUNKS:
-                quantise(chunk_source(1, i))
+            if i == 1:
+                quantise(chunk_source(1, 1))
             if i > 0:
+                banks = turn_banks if i + AHEAD < len(units) else sum_banks
                 for n in range(CHUNKS):
-                    store_chunk(*units[i - 1], n, scalar_copy)
-        store_chunk(*units[-1], 0, scalar_copy)
-        store_chunk(*units[-1], 1, vector_copy)
+                    store_chunk(*units[i - 1], n, scalar_copy, *banks)
+        store_chunk(*units[-1], 0, scalar_copy, *sum_banks)
+        store_chunk(*units[-1], 1, vector_copy, *sum_banks)

@@ -8,7 +8,6 @@ U8 = mybir.dt.uint8
 FP8X4 = mybir.dt.float8_e4m3fn_x4
 MULT = mybir.AluOpType.mult
 ADD = mybir.AluOpType.add
-SUBTRACT = mybir.AluOpType.subtract
 IDENTITY = mybir.ActivationFunctionType.Identity
 
 B, T, C, KW = 2, 1024, 512, 3
@@ -24,6 +23,7 @@ PAIR = 2 * P
 PAIRS = CHUNK // PAIR
 AHEAD = 2
 WARM = 5
+FILL = 96
 
 FLOPS = 2 * B * T * C * C + 2 * KW * B * T * C
 
@@ -39,11 +39,15 @@ def tile_cvim_pa_kernel(tc, x, w1, b1, w2, b2, out):
         tc.psum_pool(name="psum_turn", bufs=2) as psum_turn,
         tc.manual_schedule(),
     ):
-        zeros = keep.tile([P, CHUNK], BF16)
+        zeros = keep.tile([P, P], F32)
         nc.vector.memset(zeros[:], 0.0)
-        unread = psum.tile([P, CHUNK], F32, tag="bank")
+        unread = psum_turn.tile([P, P], F32, name="unread", tag="turn")
+
+        def keep_clock(width):
+            nc.tensor.matmul(out=unread[:, 0:width], lhsT=zeros[:], rhs=zeros[:, 0:width], start=True, stop=True)
+
         for k in range(WARM):
-            nc.tensor.matmul(out=unread[:], lhsT=zeros[:, 0:P], rhs=zeros[:], start=True, stop=True)
+            keep_clock(P)
 
         small_rows = keep.tile([P, (KW + 2) * P], BF16)
         nc.gpsimd.memset(small_rows[:], 0.0)
@@ -115,6 +119,8 @@ def tile_cvim_pa_kernel(tc, x, w1, b1, w2, b2, out):
         cols = keep.tile([P, KW + 2, D_BLOCKS], F32)
         tap_bias = keep.tile([P, KW, D_BLOCKS], F32)
         inner_bias = keep.tile([P, D_BLOCKS], F32)
+        ends = keep.tile([P, D_BLOCKS, 2, P], F32)
+        nc.gpsimd.memset(ends[:], 0.0)
 
         def turn_small():
             small_ps = psum.tile([P, KW + 2, P], BF16, name="small_ps", tag="bank")
@@ -132,6 +138,8 @@ def tile_cvim_pa_kernel(tc, x, w1, b1, w2, b2, out):
             nc.gpsimd.tensor_tensor(out=inner_bias[:], in0=tap_bias[:, 0, :], in1=cols[:, KW + 1, :], op=ADD)
             for j in range(1, KW):
                 nc.gpsimd.tensor_tensor(out=inner_bias[:], in0=inner_bias[:], in1=tap_bias[:, j, :], op=ADD)
+            for e, (j, col) in enumerate(((0, 0), (KW - 1, P - 1))):
+                nc.gpsimd.tensor_scalar(out=ends[:, :, e, col], in0=tap_bias[:, j, :], scalar1=-1.0, scalar2=None, op0=MULT)
 
         acc = {}
         y_cols = {}
@@ -140,30 +148,22 @@ def tile_cvim_pa_kernel(tc, x, w1, b1, w2, b2, out):
             if n == 0:
                 y_cols[b, m] = work.tile([P, T], F32, name="y_cols")
             acc[b, m, n] = psum.tile([P, CHUNK], F32, name="acc", tag="bank")
-            nc.tensor.matmul_mx(
-                out=acc[b, m, n][:],
-                lhsT=codes[W][:, m * P : (m + 1) * P].bitcast(FP8X4),
-                lhsT_scale=scales[W][:, m * P : (m + 1) * P],
-                rhs=codes[chunk_source(b, n)][:].bitcast(FP8X4),
-                rhs_scale=scales[chunk_source(b, n)][:],
-                start=True,
-                stop=True,
-            )
+            for k in range(2 if n == 0 else 1):
+                nc.tensor.matmul_mx(
+                    out=acc[b, m, n][:],
+                    lhsT=codes[W][:, m * P : (m + 1) * P].bitcast(FP8X4),
+                    lhsT_scale=scales[W][:, m * P : (m + 1) * P],
+                    rhs=codes[chunk_source(b, n)][:].bitcast(FP8X4),
+                    rhs_scale=scales[chunk_source(b, n)][:],
+                    start=True,
+                    stop=True,
+                )
             nc.scalar.activation(
                 out=y_cols[b, m][:, n * CHUNK : (n + 1) * CHUNK],
                 in_=acc[b, m, n][:],
                 func=IDENTITY,
                 scale=cols[:, 1, m : m + 1],
                 bias=inner_bias[:, m : m + 1],
-            )
-
-        def end_bias(b, m):
-            y = y_cols[b, m]
-            nc.gpsimd.tensor_tensor(
-                out=y[:, 0 : T : T - 1],
-                in0=y[:, 0 : T : T - 1],
-                in1=tap_bias[:, 0 : KW : KW - 1, m],
-                op=SUBTRACT,
             )
 
         def right_tap(b, m, n):
@@ -196,7 +196,20 @@ def tile_cvim_pa_kernel(tc, x, w1, b1, w2, b2, out):
             y_rows_ps = banks.tile([P, ROW_BLOCKS, P], F32, name="y_rows_ps", tag=tag)
             for k in range(ROW_BLOCKS):
                 t0 = n * CHUNK + k * P
-                nc.tensor.transpose(y_rows_ps[:, k, :], y_cols[b, m][:, t0 : t0 + P], ident[:])
+                parts = [y_cols[b, m][:, t0 : t0 + P]]
+                if t0 == 0:
+                    parts.insert(0, ends[:, m, 0, :])
+                if t0 + P == T:
+                    parts.insert(0, ends[:, m, 1, :])
+                for j, part in enumerate(parts):
+                    nc.tensor.matmul(
+                        out=y_rows_ps[:, k, :],
+                        lhsT=part,
+                        rhs=ident[:],
+                        is_transpose=True,
+                        start=j == 0,
+                        stop=j + 1 == len(parts),
+                    )
             y_rows = leave.tile([P, ROW_BLOCKS, P], F32)
             copy(out=y_rows[:], in_=y_rows_ps[:])
             nc.sync.dma_start(
@@ -211,12 +224,16 @@ def tile_cvim_pa_kernel(tc, x, w1, b1, w2, b2, out):
         sum_banks = (psum, "bank")
         turn_banks = (psum_turn, "turn")
         turn(W, 0, scalar_copy, *sum_banks)
-        turn_small()
+        keep_clock(FILL)
         turn(chunk_source(0, 0), 0, scalar_copy, *sum_banks)
+        keep_clock(FILL)
         turn(chunk_source(0, 0), 1, scalar_copy, *sum_banks)
+        turn_small()
+        keep_clock(FILL)
         quantise(W, 0, 1)
         for pair in range(PAIRS):
             turn(chunk_source(0, 1), pair, scalar_copy, *sum_banks)
+            keep_clock(FILL)
         quantise(chunk_source(0, 0))
         turn(W, 1, scalar_copy, *sum_banks)
         for unit in units[:AHEAD]:
@@ -234,8 +251,6 @@ def tile_cvim_pa_kernel(tc, x, w1, b1, w2, b2, out):
             if i + AHEAD < len(units):
                 for n in range(CHUNKS):
                     middle_tap(*units[i + AHEAD], n)
-                if i + AHEAD + 1 == len(units):
-                    end_bias(*units[i + AHEAD])
             if i < CHUNKS:
                 for pair in range(PAIRS):
                     turn(chunk_source(1, i), pair, scalar_copy, *turn_banks)
@@ -243,8 +258,6 @@ def tile_cvim_pa_kernel(tc, x, w1, b1, w2, b2, out):
                 right_tap(*units[i + 1], 0)
             for n in range(CHUNKS):
                 left_tap(*unit, n)
-            if i + 1 < len(units):
-                end_bias(*unit)
             if i == 1:
                 quantise(chunk_source(1, 1))
             if i > 0:

@@ -22,8 +22,7 @@ CHUNKS = T // CHUNK
 PAIR = 2 * P
 PAIRS = CHUNK // PAIR
 AHEAD = 2
-WARM = 5
-FILL = 96
+WARM = 4
 
 FLOPS = 2 * B * T * C * C + 2 * KW * B * T * C
 
@@ -43,17 +42,14 @@ def tile_cvim_pa_kernel(tc, x, w1, b1, w2, b2, out):
         nc.vector.memset(zeros[:], 0.0)
         unread = psum_turn.tile([P, P], F32, name="unread", tag="turn")
 
-        def keep_clock(width):
-            nc.tensor.matmul(out=unread[:, 0:width], lhsT=zeros[:], rhs=zeros[:, 0:width], start=True, stop=True)
+        def keep_clock():
+            nc.tensor.matmul(out=unread[:], lhsT=zeros[:], rhs=zeros[:], start=True, stop=True)
 
         for k in range(WARM):
-            keep_clock(P)
+            keep_clock()
 
         small_rows = keep.tile([P, (KW + 2) * P], BF16)
         nc.gpsimd.memset(small_rows[:], 0.0)
-        nc.scalar.dma_start(out=small_rows[0:D_BLOCKS, 0 : KW * P], in_=w2.rearrange("(m p) j -> m (p j)", p=P))
-        nc.scalar.dma_start(out=small_rows[0:D_BLOCKS, KW * P : (KW + 1) * P], in_=b1.rearrange("(m p) -> m p", p=P))
-        nc.scalar.dma_start(out=small_rows[0:D_BLOCKS, (KW + 1) * P :], in_=b2.rearrange("(m p) -> m p", p=P))
         ident = keep.tile([P, P], F32)
         make_identity(nc, ident[:])
         ident_bf = keep.tile([P, P], BF16)
@@ -82,7 +78,12 @@ def tile_cvim_pa_kernel(tc, x, w1, b1, w2, b2, out):
             )
 
         load(W, 0)
-        for n in range(CHUNKS):
+        load(chunk_source(0, 0), 0)
+        nc.sync.dma_start(out=small_rows[0:D_BLOCKS, 0 : KW * P], in_=w2.rearrange("(m p) j -> m (p j)", p=P))
+        nc.sync.dma_start(out=small_rows[0:D_BLOCKS, KW * P : (KW + 1) * P], in_=b1.rearrange("(m p) -> m p", p=P))
+        nc.sync.dma_start(out=small_rows[0:D_BLOCKS, (KW + 1) * P :], in_=b2.rearrange("(m p) -> m p", p=P))
+        load(chunk_source(0, 0), 1)
+        for n in range(1, CHUNKS):
             for pair in range(PAIRS):
                 load(chunk_source(0, n), pair)
         load(W, 1)
@@ -90,17 +91,28 @@ def tile_cvim_pa_kernel(tc, x, w1, b1, w2, b2, out):
             for pair in range(PAIRS):
                 load(chunk_source(1, n), pair)
 
+        spread_tiles = {}
+
+        def spread(k, pair):
+            spread_tiles[k, pair] = keep.tile([P, 2 * WORDS], F32, name="spread_%d_%d" % (k, pair))
+            nc.vector.tensor_copy(
+                out=spread_tiles[k, pair][:].rearrange("q (r u p) -> q r u p", r=2, u=HALVES),
+                in_=row_tiles[k][:, 2 * pair * C : (2 * pair + 2) * C]
+                .bitcast(F32)
+                .rearrange("q (r p u) -> q r u p", r=2, u=HALVES),
+            )
+
         def turn(k, pair, copy, banks, tag):
             words = row_tiles[k][:].bitcast(F32)
             flipped = banks.tile([P, HALVES, PAIR], F32, name="flipped", tag=tag)
             for r in range(2):
-                row_block = 2 * pair + r
                 for u in range(HALVES):
-                    nc.tensor.transpose(
-                        flipped[:, u, r * P : (r + 1) * P],
-                        words[:, row_block * WORDS + u : (row_block + 1) * WORDS : HALVES],
-                        ident[:],
-                    )
+                    if (k, pair) in spread_tiles:
+                        part = spread_tiles[k, pair][:, (r * HALVES + u) * P : (r * HALVES + u + 1) * P]
+                    else:
+                        row = 2 * pair + r
+                        part = words[:, row * WORDS + u : (row + 1) * WORDS : HALVES]
+                    nc.tensor.transpose(flipped[:, u, r * P : (r + 1) * P], part, ident[:])
             copy(
                 out=grouped_tiles[k][:]
                 .bitcast(F32)[:, pair * PAIR * HALVES : (pair + 1) * PAIR * HALVES]
@@ -223,19 +235,25 @@ def tile_cvim_pa_kernel(tc, x, w1, b1, w2, b2, out):
 
         sum_banks = (psum, "bank")
         turn_banks = (psum_turn, "turn")
-        turn(W, 0, scalar_copy, *sum_banks)
-        keep_clock(FILL)
-        turn(chunk_source(0, 0), 0, scalar_copy, *sum_banks)
-        keep_clock(FILL)
-        turn(chunk_source(0, 0), 1, scalar_copy, *sum_banks)
-        turn_small()
-        keep_clock(FILL)
-        quantise(W, 0, 1)
-        for pair in range(PAIRS):
-            turn(chunk_source(0, 1), pair, scalar_copy, *sum_banks)
-            keep_clock(FILL)
-        quantise(chunk_source(0, 0))
-        turn(W, 1, scalar_copy, *sum_banks)
+        early = [(W, 0)]
+        for n in range(CHUNKS):
+            for pair in range(PAIRS):
+                early.append((chunk_source(0, n), pair))
+        early.append((W, 1))
+        for i in range(2):
+            spread(*early[i])
+        for i, (k, pair) in enumerate(early):
+            turn(k, pair, scalar_copy, *sum_banks)
+            if i + 1 < len(early):
+                keep_clock()
+            if i + 2 < len(early):
+                spread(*early[i + 2])
+            if i == 1:
+                turn_small()
+            if i == 2:
+                quantise(W, 0, 1)
+            if i == 4:
+                quantise(chunk_source(0, 0))
         for unit in units[:AHEAD]:
             middle_tap(*unit, 0)
         quantise(chunk_source(0, 1))

@@ -204,6 +204,9 @@ def tile_cvim_pa_kernel(tc, x, w1, b1, w2, b2, out):
                 op1=ADD,
             )
 
+        units = [(b, m) for b in range(B) for m in range(D_BLOCKS)]
+        y_pairs = {}
+
         def store_chunk(b, m, n, copy, banks, tag):
             y_rows_ps = banks.tile([P, ROW_BLOCKS, P], F32, name="y_rows_ps", tag=tag)
             for k in range(ROW_BLOCKS):
@@ -222,16 +225,26 @@ def tile_cvim_pa_kernel(tc, x, w1, b1, w2, b2, out):
                         start=j == 0,
                         stop=j + 1 == len(parts),
                     )
-            y_rows = leave.tile([P, ROW_BLOCKS, P], F32)
-            copy(out=y_rows[:], in_=y_rows_ps[:])
+            half = m % 2
+            if half == 0:
+                y_pairs[n] = leave.tile([P, ROW_BLOCKS, 2 * P], F32, name="y_rows")
+            copy(out=y_pairs[n][:, :, half * P : (half + 1) * P], in_=y_rows_ps[:])
+            if (b, m) in units[-2:]:
+                first, width = m, 1
+            elif half == 1:
+                first, width = m - 1, 2
+            else:
+                return
+            c0 = (first % 2) * P
             nc.sync.dma_start(
-                out=out[b, n * CHUNK : (n + 1) * CHUNK, m * P : (m + 1) * P].rearrange("(k p) d -> p k d", p=P),
-                in_=y_rows[:],
+                out=out[b, n * CHUNK : (n + 1) * CHUNK, first * P : (first + width) * P].rearrange(
+                    "(k p) d -> p k d", p=P
+                ),
+                in_=y_pairs[n][:, :, c0 : c0 + width * P],
             )
 
         scalar_copy = nc.scalar.copy
         vector_copy = nc.vector.tensor_copy
-        units = [(b, m) for b in range(B) for m in range(D_BLOCKS)]
 
         sum_banks = (psum, "bank")
         turn_banks = (psum_turn, "turn")

@@ -22,7 +22,7 @@ CHUNKS = T // CHUNK
 PAIR = 2 * P
 PAIRS = CHUNK // PAIR
 AHEAD = 2
-WARM = 4
+WARM = 5
 
 FLOPS = 2 * B * T * C * C + 2 * KW * B * T * C
 
@@ -77,19 +77,13 @@ def tile_cvim_pa_kernel(tc, x, w1, b1, w2, b2, out):
                 in_=drams[k][pair * PAIR : (pair + 1) * PAIR, :].rearrange("(p r) c -> p (r c)", r=2),
             )
 
-        load(W, 0)
-        load(chunk_source(0, 0), 0)
-        nc.sync.dma_start(out=small_rows[0:D_BLOCKS, 0 : KW * P], in_=w2.rearrange("(m p) j -> m (p j)", p=P))
-        nc.sync.dma_start(out=small_rows[0:D_BLOCKS, KW * P : (KW + 1) * P], in_=b1.rearrange("(m p) -> m p", p=P))
-        nc.sync.dma_start(out=small_rows[0:D_BLOCKS, (KW + 1) * P :], in_=b2.rearrange("(m p) -> m p", p=P))
-        load(chunk_source(0, 0), 1)
-        for n in range(1, CHUNKS):
-            for pair in range(PAIRS):
-                load(chunk_source(0, n), pair)
-        load(W, 1)
-        for n in range(CHUNKS):
-            for pair in range(PAIRS):
-                load(chunk_source(1, n), pair)
+        pairs = [(k, pair) for k in range(1 + B * CHUNKS) for pair in range(PAIRS)]
+        for i, (k, pair) in enumerate(pairs):
+            if i == 2:
+                nc.sync.dma_start(out=small_rows[0:D_BLOCKS, 0 : KW * P], in_=w2.rearrange("(m p) j -> m (p j)", p=P))
+                nc.sync.dma_start(out=small_rows[0:D_BLOCKS, KW * P : (KW + 1) * P], in_=b1.rearrange("(m p) -> m p", p=P))
+                nc.sync.dma_start(out=small_rows[0:D_BLOCKS, (KW + 1) * P :], in_=b2.rearrange("(m p) -> m p", p=P))
+            load(k, pair)
 
         spread_tiles = {}
 
@@ -248,11 +242,7 @@ def tile_cvim_pa_kernel(tc, x, w1, b1, w2, b2, out):
 
         sum_banks = (psum, "bank")
         turn_banks = (psum_turn, "turn")
-        early = [(W, 0)]
-        for n in range(CHUNKS):
-            for pair in range(PAIRS):
-                early.append((chunk_source(0, n), pair))
-        early.append((W, 1))
+        early = pairs[:-PAIRS]
         for i in range(2):
             spread(*early[i])
         for i, (k, pair) in enumerate(early):
@@ -263,34 +253,27 @@ def tile_cvim_pa_kernel(tc, x, w1, b1, w2, b2, out):
                 spread(*early[i + 2])
             if i == 1:
                 turn_small()
-            if i == 2:
-                quantise(W, 0, 1)
-            if i == 4:
-                quantise(chunk_source(0, 0))
+            if k > 0 and pair == 0:
+                quantise(k - 1)
         for unit in units[:AHEAD]:
-            middle_tap(*unit, 0)
-        quantise(chunk_source(0, 1))
-        for unit in units[:AHEAD]:
-            middle_tap(*unit, 1)
+            for n in range(CHUNKS):
+                middle_tap(*unit, n)
+        for pair in range(PAIRS):
+            turn(chunk_source(B - 1, CHUNKS - 1), pair, scalar_copy, *turn_banks)
         right_tap(*units[0], 0)
-        quantise(W, 1, 1)
+        quantise(chunk_source(B - 1, 0))
 
         for i, unit in enumerate(units):
             right_tap(*unit, 1)
-            if i == 1:
-                quantise(chunk_source(1, 0))
             if i + AHEAD < len(units):
                 for n in range(CHUNKS):
                     middle_tap(*units[i + AHEAD], n)
-            if i < CHUNKS:
-                for pair in range(PAIRS):
-                    turn(chunk_source(1, i), pair, scalar_copy, *turn_banks)
             if i + 1 < len(units):
                 right_tap(*units[i + 1], 0)
             for n in range(CHUNKS):
                 left_tap(*unit, n)
-            if i == 1:
-                quantise(chunk_source(1, 1))
+            if i == 0:
+                quantise(chunk_source(B - 1, CHUNKS - 1))
             if i > 0:
                 banks = turn_banks if i + AHEAD < len(units) else sum_banks
                 for n in range(CHUNKS):

@@ -21,6 +21,10 @@ D_BLOCKS = C // P
 CHUNKS = T // CHUNK
 PAIR = 2 * P
 PAIRS = CHUNK // PAIR
+EDGE = 8
+TAIL = ()
+FARN = 1
+V61 = 1
 AHEAD = 2
 WARM = 5
 
@@ -42,11 +46,11 @@ def tile_cvim_pa_kernel(tc, x, w1, b1, w2, b2, out):
         nc.vector.memset(zeros[:], 0.0)
         unread = psum_turn.tile([P, P], F32, name="unread", tag="turn")
 
-        def keep_clock():
-            nc.tensor.matmul(out=unread[:], lhsT=zeros[:], rhs=zeros[:], start=True, stop=True)
+        def keep_clock(bank):
+            nc.tensor.matmul(out=bank, lhsT=zeros[:], rhs=zeros[:], start=True, stop=True)
 
         for k in range(WARM):
-            keep_clock()
+            keep_clock(unread[:])
 
         small_rows = keep.tile([P, (KW + 2) * P], BF16)
         nc.gpsimd.memset(small_rows[:], 0.0)
@@ -77,9 +81,10 @@ def tile_cvim_pa_kernel(tc, x, w1, b1, w2, b2, out):
                 in_=drams[k][pair * PAIR : (pair + 1) * PAIR, :].rearrange("(p r) c -> p (r c)", r=2),
             )
 
-        pairs = [(k, pair) for k in range(1 + B * CHUNKS) for pair in range(PAIRS)]
+        pairs = [(W, 0), (chunk_source(0, 0), 0), (chunk_source(0, 0), 1), (W, 1)]
+        pairs += [(k, pair) for k in range(chunk_source(0, 1), 1 + B * CHUNKS) for pair in range(PAIRS)]
         for i, (k, pair) in enumerate(pairs):
-            if i == 2:
+            if i == 1:
                 nc.sync.dma_start(out=small_rows[0:D_BLOCKS, 0 : KW * P], in_=w2.rearrange("(m p) j -> m (p j)", p=P))
                 nc.sync.dma_start(out=small_rows[0:D_BLOCKS, KW * P : (KW + 1) * P], in_=b1.rearrange("(m p) -> m p", p=P))
                 nc.sync.dma_start(out=small_rows[0:D_BLOCKS, (KW + 1) * P :], in_=b2.rearrange("(m p) -> m p", p=P))
@@ -154,22 +159,34 @@ def tile_cvim_pa_kernel(tc, x, w1, b1, w2, b2, out):
             if n == 0:
                 y_cols[b, m] = work.tile([P, T], F32, name="y_cols")
             acc[b, m, n] = psum.tile([P, CHUNK], F32, name="acc", tag="bank")
-            for k in range(2 if n == 0 else 1):
-                nc.tensor.matmul_mx(
-                    out=acc[b, m, n][:],
-                    lhsT=codes[W][:, m * P : (m + 1) * P].bitcast(FP8X4),
-                    lhsT_scale=scales[W][:, m * P : (m + 1) * P],
-                    rhs=codes[chunk_source(b, n)][:].bitcast(FP8X4),
-                    rhs_scale=scales[chunk_source(b, n)][:],
-                    start=True,
-                    stop=True,
-                )
+            for k in range(2 if n == 0 and units.index((b, m)) >= AHEAD else 1):
+              nc.tensor.matmul_mx(
+                out=acc[b, m, n][:],
+                lhsT=codes[W][:, m * P : (m + 1) * P].bitcast(FP8X4),
+                lhsT_scale=scales[W][:, m * P : (m + 1) * P],
+                rhs=codes[chunk_source(b, n)][:].bitcast(FP8X4),
+                rhs_scale=scales[chunk_source(b, n)][:],
+                start=True,
+                stop=True,
+            )
             nc.scalar.activation(
                 out=y_cols[b, m][:, n * CHUNK : (n + 1) * CHUNK],
                 in_=acc[b, m, n][:],
                 func=IDENTITY,
                 scale=cols[:, 1, m : m + 1],
                 bias=inner_bias[:, m : m + 1],
+            )
+
+        far = keep.tile([P, FARN * CHUNK + EDGE], F32)
+        nc.gpsimd.memset(far[:, FARN * CHUNK :], 0.0)
+
+        def far_product(b, m, n):
+            nc.scalar.activation(
+                out=far[:, n * CHUNK : (n + 1) * CHUNK],
+                in_=acc[b, m, n][:],
+                func=IDENTITY,
+                scale=cols[:, 2, m : m + 1],
+                bias=0.0,
             )
 
         def right_tap(b, m, n):
@@ -201,11 +218,14 @@ def tile_cvim_pa_kernel(tc, x, w1, b1, w2, b2, out):
         units = [(b, m) for b in range(B) for m in range(D_BLOCKS)]
         y_pairs = {}
 
-        def store_chunk(b, m, n, copy, banks, tag):
-            y_rows_ps = banks.tile([P, ROW_BLOCKS, P], F32, name="y_rows_ps", tag=tag)
-            for k in range(ROW_BLOCKS):
-                t0 = n * CHUNK + k * P
+        def store_chunk(b, m, n, copy, banks, tag, first_block=0, blocks=ROW_BLOCKS, queue=nc.sync):
+            y_rows_ps = banks.tile([P, blocks, P], F32, name="y_rows_ps", tag=tag)
+            t_first = n * CHUNK + first_block * P
+            for k in range(blocks):
+                t0 = t_first + k * P
                 parts = [y_cols[b, m][:, t0 : t0 + P]]
+                if (b, m) == units[-1] and n < FARN:
+                    parts.insert(0, far[:, t0 + 1 : t0 + 1 + P])
                 if t0 == 0:
                     parts.insert(0, ends[:, m, 0, :])
                 if t0 + P == T:
@@ -220,21 +240,22 @@ def tile_cvim_pa_kernel(tc, x, w1, b1, w2, b2, out):
                         stop=j + 1 == len(parts),
                     )
             half = m % 2
-            if half == 0:
+            if (half == 0 and first_block == 0) or ((b, m) == units[-1] and first_block == 0):
                 y_pairs[n] = leave.tile([P, ROW_BLOCKS, 2 * P], F32, name="y_rows")
-            copy(out=y_pairs[n][:, :, half * P : (half + 1) * P], in_=y_rows_ps[:])
-            if (b, m) in units[-2:]:
+            rows = slice(first_block, first_block + blocks)
+            copy(out=y_pairs[n][:, rows, half * P : (half + 1) * P], in_=y_rows_ps[:])
+            if b == B - 1 or m < 2:
                 first, width = m, 1
             elif half == 1:
                 first, width = m - 1, 2
             else:
                 return
             c0 = (first % 2) * P
-            nc.sync.dma_start(
-                out=out[b, n * CHUNK : (n + 1) * CHUNK, first * P : (first + width) * P].rearrange(
+            queue.dma_start(
+                out=out[b, t_first : t_first + blocks * P, first * P : (first + width) * P].rearrange(
                     "(k p) d -> p k d", p=P
                 ),
-                in_=y_pairs[n][:, :, c0 : c0 + width * P],
+                in_=y_pairs[n][:, rows, c0 : c0 + width * P],
             )
 
         scalar_copy = nc.scalar.copy
@@ -242,41 +263,70 @@ def tile_cvim_pa_kernel(tc, x, w1, b1, w2, b2, out):
 
         sum_banks = (psum, "bank")
         turn_banks = (psum_turn, "turn")
-        early = pairs[:-PAIRS]
         for i in range(2):
-            spread(*early[i])
-        for i, (k, pair) in enumerate(early):
-            turn(k, pair, scalar_copy, *sum_banks)
-            if i + 1 < len(early):
-                keep_clock()
-            if i + 2 < len(early):
-                spread(*early[i + 2])
+            spread(*pairs[i])
+        for i, (k, pair) in enumerate(pairs[:6]):
+            if i + 2 < 5:
+                spread(*pairs[i + 2])
+            if i == 3:
+                quantise(W, 0, 1)
+            if i == 5:
+                quantise(chunk_source(0, 0))
+            turn(k, pair, vector_copy if i == 3 else scalar_copy, *sum_banks)
             if i == 1:
                 turn_small()
-            if k > 0 and pair == 0:
-                quantise(k - 1)
-        for unit in units[:AHEAD]:
-            for n in range(CHUNKS):
-                middle_tap(*unit, n)
-        for pair in range(PAIRS):
-            turn(chunk_source(B - 1, CHUNKS - 1), pair, scalar_copy, *turn_banks)
+            if i == 0:
+                keep_clock(unread[:])
+        middle_tap(*units[0], 0)
+        middle_tap(*units[1], 0)
+        quantise(chunk_source(0, 1))
         right_tap(*units[0], 0)
-        quantise(chunk_source(B - 1, 0))
+        right_tap(*units[1], 0)
+        middle_tap(*units[0], 1)
+        middle_tap(*units[1], 1)
+        turn(*pairs[6], scalar_copy, *turn_banks)
+        turn(*pairs[7], scalar_copy, *turn_banks)
 
         for i, unit in enumerate(units):
-            right_tap(*unit, 1)
+            after = units[i + 1] if i + 1 < len(units) else None
+            if after:
+                right_tap(*unit, 1)
+            if i == 0:
+                quantise(W, 1, 1)
             if i + AHEAD < len(units):
                 for n in range(CHUNKS):
                     middle_tap(*units[i + AHEAD], n)
-            if i + 1 < len(units):
-                right_tap(*units[i + 1], 0)
-            for n in range(CHUNKS):
-                left_tap(*unit, n)
+                    if units[i + AHEAD] == units[-1] and n < FARN:
+                        far_product(*units[-1], n)
+            if after == units[-1]:
+                left_tap(*after, 0)
+                left_tap(*unit, 0)
+                if FARN == 1:
+                    right_tap(*after, 1)
+            elif after:
+                if i > 0:
+                    right_tap(*after, 0)
+                left_tap(*unit, 0)
+            left_tap(*unit, 1)
+            if i < CHUNKS:
+                quantise(chunk_source(1, i))
             if i == 0:
-                quantise(chunk_source(B - 1, CHUNKS - 1))
-            if i > 0:
+                for pair in range(PAIRS):
+                    turn(chunk_source(1, 1), pair, scalar_copy, *turn_banks)
+            if i + 2 == len(units):
+                tail_clock = psum_turn.tile([P, P], F32, name="tail_clock", tag="turn")
+            if 0 < i < len(units) - 1:
                 banks = turn_banks if i + AHEAD < len(units) else sum_banks
                 for n in range(CHUNKS):
                     store_chunk(*units[i - 1], n, scalar_copy, *banks)
+                    if i in TAIL:
+                        keep_clock(tail_clock[:])
         store_chunk(*units[-1], 0, scalar_copy, *sum_banks)
-        store_chunk(*units[-1], 1, vector_copy, *sum_banks)
+        if 7 in TAIL:
+            keep_clock(tail_clock[:])
+        store_chunk(*units[-2], 0, scalar_copy, *sum_banks)
+        if 8 in TAIL:
+            keep_clock(tail_clock[:])
+        store_chunk(*units[-2], 1, vector_copy if V61 else scalar_copy, *sum_banks)
+        store_chunk(*units[-1], 1, vector_copy, *sum_banks, 0, ROW_BLOCKS // 2)
+        store_chunk(*units[-1], 1, scalar_copy, *sum_banks, ROW_BLOCKS // 2, ROW_BLOCKS // 2, nc.scalar)

from concourse import mybir
from concourse.masks import make_identity

F32 = mybir.dt.float32
BF16 = mybir.dt.bfloat16
U32 = mybir.dt.uint32
U8 = mybir.dt.uint8
FP8X4 = mybir.dt.float8_e4m3fn_x4
MULT = mybir.AluOpType.mult
ADD = mybir.AluOpType.add
IDENTITY = mybir.ActivationFunctionType.Identity

B, T, C, KW = 2, 1024, 512, 3
P = 128
PACK = 4
HALVES = 2
WORDS = C // 2
CHUNK = 512
ROW_BLOCKS = CHUNK // P
D_BLOCKS = C // P
CHUNKS = T // CHUNK
PAIR = 2 * P
PAIRS = CHUNK // PAIR
EDGE = 8
TAIL = ()
FARN = 1
V61 = 1
AHEAD = 2
WARM = 5

FLOPS = 2 * B * T * C * C + 2 * KW * B * T * C


def tile_cvim_pa_kernel(tc, x, w1, b1, w2, b2, out):
    nc = tc.nc

    with (
        tc.tile_pool(name="keep", bufs=1) as keep,
        tc.tile_pool(name="work", bufs=AHEAD + 3) as work,
        tc.tile_pool(name="leave", bufs=8) as leave,
        tc.psum_pool(name="psum", bufs=(AHEAD + 1) * CHUNKS) as psum,
        tc.psum_pool(name="psum_turn", bufs=2) as psum_turn,
        tc.manual_schedule(),
    ):
        zeros = keep.tile([P, P], F32)
        nc.vector.memset(zeros[:], 0.0)
        unread = psum_turn.tile([P, P], F32, name="unread", tag="turn")

        def keep_clock(bank):
            nc.tensor.matmul(out=bank, lhsT=zeros[:], rhs=zeros[:], start=True, stop=True)

        for k in range(WARM):
            keep_clock(unread[:])

        small_rows = keep.tile([P, (KW + 2) * P], BF16)
        nc.gpsimd.memset(small_rows[:], 0.0)
        ident = keep.tile([P, P], F32)
        make_identity(nc, ident[:])
        ident_bf = keep.tile([P, P], BF16)
        nc.vector.tensor_copy(out=ident_bf[:], in_=ident[:])

        W = 0

        def chunk_source(b, n):
            return 1 + CHUNKS * b + n

        row_tiles, grouped_tiles, codes, scales, drams = [], [], [], [], []
        for k in range(1 + B * CHUNKS):
            row_tiles.append(keep.tile([P, ROW_BLOCKS * C], BF16, name="rows_%d" % k))
            grouped_tiles.append(keep.tile([P, CHUNK * PACK], BF16, align_bytes=64, name="grouped_%d" % k))
            codes.append(keep.tile([P, CHUNK], U32, align_bytes=64, name="codes_%d" % k))
            scales.append(keep.tile([P, CHUNK], U8, align_bytes=64, name="scales_%d" % k))
        drams.append(w1)
        for b in range(B):
            for n in range(CHUNKS):
                drams.append(x[b, n * CHUNK : (n + 1) * CHUNK, :])

        def load(k, pair):
            nc.sync.dma_start(
                out=row_tiles[k][:, 2 * pair * C : (2 * pair + 2) * C],
                in_=drams[k][pair * PAIR : (pair + 1) * PAIR, :].rearrange("(p r) c -> p (r c)", r=2),
            )

        pairs = [(W, 0), (chunk_source(0, 0), 0), (chunk_source(0, 0), 1), (W, 1)]
        pairs += [(k, pair) for k in range(chunk_source(0, 1), 1 + B * CHUNKS) for pair in range(PAIRS)]
        for i, (k, pair) in enumerate(pairs):
            if i == 1:
                nc.sync.dma_start(out=small_rows[0:D_BLOCKS, 0 : KW * P], in_=w2.rearrange("(m p) j -> m (p j)", p=P))
                nc.sync.dma_start(out=small_rows[0:D_BLOCKS, KW * P : (KW + 1) * P], in_=b1.rearrange("(m p) -> m p", p=P))
                nc.sync.dma_start(out=small_rows[0:D_BLOCKS, (KW + 1) * P :], in_=b2.rearrange("(m p) -> m p", p=P))
            load(k, pair)

        spread_tiles = {}

        def spread(k, pair):
            spread_tiles[k, pair] = keep.tile([P, 2 * WORDS], F32, name="spread_%d_%d" % (k, pair))
            nc.vector.tensor_copy(
                out=spread_tiles[k, pair][:].rearrange("q (r u p) -> q r u p", r=2, u=HALVES),
                in_=row_tiles[k][:, 2 * pair * C : (2 * pair + 2) * C]
                .bitcast(F32)
                .rearrange("q (r p u) -> q r u p", r=2, u=HALVES),
            )

        def turn(k, pair, copy, banks, tag):
            words = row_tiles[k][:].bitcast(F32)
            flipped = banks.tile([P, HALVES, PAIR], F32, name="flipped", tag=tag)
            for r in range(2):
                for u in range(HALVES):
                    if (k, pair) in spread_tiles:
                        part = spread_tiles[k, pair][:, (r * HALVES + u) * P : (r * HALVES + u + 1) * P]
                    else:
                        row = 2 * pair + r
                        part = words[:, row * WORDS + u : (row + 1) * WORDS : HALVES]
                    nc.tensor.transpose(flipped[:, u, r * P : (r + 1) * P], part, ident[:])
            copy(
                out=grouped_tiles[k][:]
                .bitcast(F32)[:, pair * PAIR * HALVES : (pair + 1) * PAIR * HALVES]
                .rearrange("p (t r u) -> p t r u", r=2, u=HALVES),
                in_=flipped[:].rearrange("p u (r t) -> p t r u", r=2),
            )

        def quantise(k, first_pair=0, pairs=PAIRS):
            rows = slice(first_pair * PAIR, (first_pair + pairs) * PAIR)
            nc.vector.quantize_mx(
                out=codes[k][:, rows].bitcast(FP8X4),
                scales=scales[k][:, rows],
                in_=grouped_tiles[k][:, rows.start * PACK : rows.stop * PACK],
            )

        cols = keep.tile([P, KW + 2, D_BLOCKS], F32)
        tap_bias = keep.tile([P, KW, D_BLOCKS], F32)
        inner_bias = keep.tile([P, D_BLOCKS], F32)
        ends = keep.tile([P, D_BLOCKS, 2, P], F32)
        nc.gpsimd.memset(ends[:], 0.0)

        def turn_small():
            small_ps = psum.tile([P, KW + 2, P], BF16, name="small_ps", tag="bank")
            views = [small_rows[:, j : KW * P : KW] for j in range(KW)]
            views += [small_rows[:, KW * P : (KW + 1) * P], small_rows[:, (KW + 1) * P :]]
            for j, view in enumerate(views):
                nc.tensor.transpose(small_ps[:, j, :], view, ident_bf[:])
            nc.vector.tensor_copy(out=cols[:], in_=small_ps[:, :, 0:D_BLOCKS])
            nc.gpsimd.tensor_tensor(
                out=tap_bias[:],
                in0=cols[:, 0:KW, :],
                in1=cols[:, KW : KW + 1, :].to_broadcast([P, KW, D_BLOCKS]),
                op=MULT,
            )
            nc.gpsimd.tensor_tensor(out=inner_bias[:], in0=tap_bias[:, 0, :], in1=cols[:, KW + 1, :], op=ADD)
            for j in range(1, KW):
                nc.gpsimd.tensor_tensor(out=inner_bias[:], in0=inner_bias[:], in1=tap_bias[:, j, :], op=ADD)
            for e, (j, col) in enumerate(((0, 0), (KW - 1, P - 1))):
                nc.gpsimd.tensor_scalar(out=ends[:, :, e, col], in0=tap_bias[:, j, :], scalar1=-1.0, scalar2=None, op0=MULT)

        acc = {}
        y_cols = {}

        def middle_tap(b, m, n):
            if n == 0:
                y_cols[b, m] = work.tile([P, T], F32, name="y_cols")
            acc[b, m, n] = psum.tile([P, CHUNK], F32, name="acc", tag="bank")
            for k in range(2 if n == 0 and units.index((b, m)) >= AHEAD else 1):
              nc.tensor.matmul_mx(
                out=acc[b, m, n][:],
                lhsT=codes[W][:, m * P : (m + 1) * P].bitcast(FP8X4),
                lhsT_scale=scales[W][:, m * P : (m + 1) * P],
                rhs=codes[chunk_source(b, n)][:].bitcast(FP8X4),
                rhs_scale=scales[chunk_source(b, n)][:],
                start=True,
                stop=True,
            )
            nc.scalar.activation(
                out=y_cols[b, m][:, n * CHUNK : (n + 1) * CHUNK],
                in_=acc[b, m, n][:],
                func=IDENTITY,
                scale=cols[:, 1, m : m + 1],
                bias=inner_bias[:, m : m + 1],
            )

        far = keep.tile([P, FARN * CHUNK + EDGE], F32)
        nc.gpsimd.memset(far[:, FARN * CHUNK :], 0.0)

        def far_product(b, m, n):
            nc.scalar.activation(
                out=far[:, n * CHUNK : (n + 1) * CHUNK],
                in_=acc[b, m, n][:],
                func=IDENTITY,
                scale=cols[:, 2, m : m + 1],
                bias=0.0,
            )

        def right_tap(b, m, n):
            y = y_cols[b, m]
            t0 = n * CHUNK
            skip = 1 if n == 0 else 0
            nc.vector.scalar_tensor_tensor(
                out=y[:, t0 - 1 + skip : t0 + CHUNK - 1],
                in0=acc[b, m, n][:, skip:CHUNK],
                scalar=cols[:, 2, m : m + 1],
                in1=y[:, t0 - 1 + skip : t0 + CHUNK - 1],
                op0=MULT,
                op1=ADD,
            )

        def left_tap(b, m, n):
            y = y_cols[b, m]
            t0 = n * CHUNK
            width = min(CHUNK, T - 1 - t0)
            nc.vector.scalar_tensor_tensor(
                out=y[:, t0 + 1 : t0 + 1 + width],
                in0=acc[b, m, n][:, 0:width],
                scalar=cols[:, 0, m : m + 1],
                in1=y[:, t0 + 1 : t0 + 1 + width],
                op0=MULT,
                op1=ADD,
            )

        units = [(b, m) for b in range(B) for m in range(D_BLOCKS)]
        y_pairs = {}

        def store_chunk(b, m, n, copy, banks, tag, first_block=0, blocks=ROW_BLOCKS, queue=nc.sync):
            y_rows_ps = banks.tile([P, blocks, P], F32, name="y_rows_ps", tag=tag)
            t_first = n * CHUNK + first_block * P
            for k in range(blocks):
                t0 = t_first + k * P
                parts = [y_cols[b, m][:, t0 : t0 + P]]
                if (b, m) == units[-1] and n < FARN:
                    parts.insert(0, far[:, t0 + 1 : t0 + 1 + P])
                if t0 == 0:
                    parts.insert(0, ends[:, m, 0, :])
                if t0 + P == T:
                    parts.insert(0, ends[:, m, 1, :])
                for j, part in enumerate(parts):
                    nc.tensor.matmul(
                        out=y_rows_ps[:, k, :],
                        lhsT=part,
                        rhs=ident[:],
                        is_transpose=True,
                        start=j == 0,
                        stop=j + 1 == len(parts),
                    )
            half = m % 2
            if (half == 0 and first_block == 0) or ((b, m) == units[-1] and first_block == 0):
                y_pairs[n] = leave.tile([P, ROW_BLOCKS, 2 * P], F32, name="y_rows")
            rows = slice(first_block, first_block + blocks)
            copy(out=y_pairs[n][:, rows, half * P : (half + 1) * P], in_=y_rows_ps[:])
            if b == B - 1 or m < 2:
                first, width = m, 1
            elif half == 1:
                first, width = m - 1, 2
            else:
                return
            c0 = (first % 2) * P
            queue.dma_start(
                out=out[b, t_first : t_first + blocks * P, first * P : (first + width) * P].rearrange(
                    "(k p) d -> p k d", p=P
                ),
                in_=y_pairs[n][:, rows, c0 : c0 + width * P],
            )

        scalar_copy = nc.scalar.copy
        vector_copy = nc.vector.tensor_copy

        sum_banks = (psum, "bank")
        turn_banks = (psum_turn, "turn")
        for i in range(2):
            spread(*pairs[i])
        for i, (k, pair) in enumerate(pairs[:6]):
            if i + 2 < 5:
                spread(*pairs[i + 2])
            if i == 3:
                quantise(W, 0, 1)
            if i == 5:
                quantise(chunk_source(0, 0))
            turn(k, pair, vector_copy if i == 3 else scalar_copy, *sum_banks)
            if i == 1:
                turn_small()
            if i == 0:
                keep_clock(unread[:])
        middle_tap(*units[0], 0)
        middle_tap(*units[1], 0)
        quantise(chunk_source(0, 1))
        right_tap(*units[0], 0)
        right_tap(*units[1], 0)
        middle_tap(*units[0], 1)
        middle_tap(*units[1], 1)
        turn(*pairs[6], scalar_copy, *turn_banks)
        turn(*pairs[7], scalar_copy, *turn_banks)

        for i, unit in enumerate(units):
            after = units[i + 1] if i + 1 < len(units) else None
            if after:
                right_tap(*unit, 1)
            if i == 0:
                quantise(W, 1, 1)
            if i + AHEAD < len(units):
                for n in range(CHUNKS):
                    middle_tap(*units[i + AHEAD], n)
                    if units[i + AHEAD] == units[-1] and n < FARN:
                        far_product(*units[-1], n)
            if after == units[-1]:
                left_tap(*after, 0)
                left_tap(*unit, 0)
                if FARN == 1:
                    right_tap(*after, 1)
            elif after:
                if i > 0:
                    right_tap(*after, 0)
                left_tap(*unit, 0)
            left_tap(*unit, 1)
            if i < CHUNKS:
                quantise(chunk_source(1, i))
            if i == 0:
                for pair in range(PAIRS):
                    turn(chunk_source(1, 1), pair, scalar_copy, *turn_banks)
            if i + 2 == len(units):
                tail_clock = psum_turn.tile([P, P], F32, name="tail_clock", tag="turn")
            if 0 < i < len(units) - 1:
                banks = turn_banks if i + AHEAD < len(units) else sum_banks
                for n in range(CHUNKS):
                    store_chunk(*units[i - 1], n, scalar_copy, *banks)
                    if i in TAIL:
                        keep_clock(tail_clock[:])
        store_chunk(*units[-1], 0, scalar_copy, *sum_banks)
        if 7 in TAIL:
            keep_clock(tail_clock[:])
        store_chunk(*units[-2], 0, scalar_copy, *sum_banks)
        if 8 in TAIL:
            keep_clock(tail_clock[:])
        store_chunk(*units[-2], 1, vector_copy if V61 else scalar_copy, *sum_banks)
        store_chunk(*units[-1], 1, vector_copy, *sum_banks, 0, ROW_BLOCKS // 2)
        store_chunk(*units[-1], 1, scalar_copy, *sum_banks, ROW_BLOCKS // 2, ROW_BLOCKS // 2, nc.scalar)
